import numpy as np
import ml_dtypes


def mxq(x, axis, fmt="e4m3"):
    dtype, down = {"e4m3": (ml_dtypes.float8_e4m3fn, 7), "e5m2": (ml_dtypes.float8_e5m2, 14)}[fmt]
    v = np.moveaxis(np.asarray(x, np.float32).astype(ml_dtypes.bfloat16).astype(np.float64), axis, -1)
    blocks = v.reshape(v.shape[:-1] + (-1, 32))
    amax = np.abs(blocks).max(-1, keepdims=True)
    byte = np.maximum(np.where(amax > 0, np.frexp(amax)[1] - 1 + 127, 0) - down, 1)
    scale = np.exp2(byte - 127.0)
    codes = (blocks / scale).astype(np.float32).astype(dtype).astype(np.float64)
    return np.moveaxis((codes * scale).reshape(v.shape), -1, axis)


WIDE = False


def mx_kscale(k):
    if not WIDE:
        return np.ones(k)
    levels = np.array([10, -10, 5, -5, 0])
    if k % 512:
        return np.exp2(np.random.permutation(np.resize(levels, k // 32))).repeat(32)
    a = np.empty((k // 512, 16))
    for p in range(k // 512):
        a[p, :8] = np.random.permutation(np.resize(levels, 8))
        for g in range(8):
            far = levels[np.abs(levels - a[p, g]) >= 10]
            a[p, g + 8] = far[np.random.randint(len(far))]
    return np.exp2(a.ravel()).repeat(32)


BF16 = ml_dtypes.bfloat16


def bf(x):
    return np.asarray(x, np.float32).astype(BF16)


def f64(x):
    return np.asarray(x).astype(np.float64)


N, K, D_IN, HC, H = 256, 8, 1024, 1024, 1024


def sigmoid(v):
    return 1.0 / (1.0 + np.exp(-v))


def setup_inputs():
    s, t = mx_kscale(D_IN), mx_kscale(HC)
    return {
        "x": bf(np.random.standard_normal((N, D_IN)) * s),
        "child_h": bf(np.random.standard_normal((N, K, HC)) * t),
        "child_c": bf(np.random.standard_normal((N, K, H)) * 0.5),
        "Wf": bf(np.random.standard_normal((D_IN, H)) * 0.7 / np.sqrt(D_IN) / s[:, None]),
        "bWf": bf(np.random.standard_normal(H) * 0.3),
        "Uf": bf(np.random.standard_normal((HC, H)) * 0.7 / np.sqrt(HC) / t[:, None]),
        "bUf": bf(np.random.standard_normal(H) * 0.3),
    }


def core(x, child_h, child_c, Wf, bWf, Uf, bUf):
    xf = (mxq(f64(x), 1, "e4m3") @ mxq(f64(Wf), 0, "e4m3")) + f64(bWf)
    hf = mxq(f64(child_h), 2, "e4m3") @ mxq(f64(Uf), 0, "e4m3")
    f = sigmoid(xf[:, None, :] + hf + f64(bUf))
    return (f * f64(child_c)).sum(axis=1)


def e4m3fn_bytes(y):
    return np.clip(np.asarray(y, np.float64), -448.0, 448.0).astype(np.float32).astype(ml_dtypes.float8_e4m3fn).view(np.uint8)


Y_SCALE = 270.0


def reference(x, child_h, child_c, Wf, bWf, Uf, bUf):
    out = core(x, child_h, child_c, Wf, bWf, Uf, bUf)
    return out, e4m3fn_bytes(out * Y_SCALE)

@@ -1,0 +1,440 @@
+from contextlib import ExitStack
+
+import concourse.mybir as mybir
+from concourse.masks import make_identity
+
+FLOPS = 2 * 2048 * 1024 * 1024 + 2 * 256 * 1024 * 1024
+
+F32 = mybir.dt.float32
+BF16 = mybir.dt.bfloat16
+U32 = mybir.dt.uint32
+U8 = mybir.dt.uint8
+FP8X4 = mybir.dt.float8_e4m3fn_x4
+FP8 = mybir.dt.float8_e4m3fn
+ALU = mybir.AluOpType
+ACT = mybir.ActivationFunctionType
+
+P = 128
+KP = 4
+G = 2
+HW = 512
+Y_SCALE = 270.0
+NSTEP = 16
+
+HEAD_SPLIT = [256,256,0]
+LATE_SPLIT = [192,320,0]
+LATE_PIECE = 512
+G_PROD = True
+HEAD_EVAC_V = False
+ACC_BUFS = 3
+F1_STEPS = 3
+ZT_BUFS = 9
+LAG = 1
+G_FROM = 0
+PF = 3
+COPY4 = True
+V_COLS = 320
+FAST_TAIL = True
+PE_LATE = False
+PE_EVAC = ["v","v"]
+G_BUSY = [i - LAG for i in range(3, 7)] if LATE_SPLIT[2] > 0 else []
+QF = 2
+F2_DELAY = 1
+H_BUFS = 6
+
+
+def tile_childsumtreelstmcell_pa_kernel(tc, x, child_h, child_c, Wf, bWf, Uf, bUf, out_0, out_1):
+    nc = tc.nc
+    with ExitStack() as ctx:
+        const = ctx.enter_context(tc.tile_pool(name="const", bufs=1))
+        raw = ctx.enter_context(tc.tile_pool(name="raw", bufs=1))
+        grp = ctx.enter_context(tc.tile_pool(name="grp", bufs=3))
+        codes = ctx.enter_context(tc.tile_pool(name="codes", bufs=1))
+        ep = ctx.enter_context(tc.tile_pool(name="ep", bufs=2))
+        psum = ctx.enter_context(tc.psum_pool(name="psum", bufs=1))
+        ctx.enter_context(tc.manual_schedule())
+
+        ident = const.tile([P, P], F32, name="ident")
+        make_identity(nc, ident[:])
+        ones = const.tile([P, P], BF16, name="ones")
+        nc.vector.memset(ones[:], 1.0)
+        brow = const.tile([P, 2 * HW], BF16, name="brow")
+        nc.gpsimd.memset(brow[:], 0.0)
+        warm = const.tile([P, 2], F32, name="warm")
+        nc.vector.memset(warm[:], 0.0)
+        nc.scalar.activation(out=warm[:, 1:2], in_=warm[:, 0:1], func=ACT.Sigmoid)
+        gdum = const.tile([P, NSTEP + 2], F32, name="gdum")
+
+        x_raw = {}
+        w_raw = {}
+        h_raw = {}
+        c_raw = {}
+        W = {0: Wf, 1: Uf}
+
+        def load_x(t):
+            x_raw[t] = raw.tile([P, 1024], BF16, name="x_raw%d" % t)
+            nc.sync.dma_start(out=x_raw[t][:], in_=x[t * P:(t + 1) * P, :])
+
+        def load_w(m, g, hh):
+            w_raw[(m, g, hh)] = raw.tile([P, 4, HW], BF16, name="w_raw%d%d%d" % (m, g, hh))
+            nc.sync.dma_start(
+                out=w_raw[(m, g, hh)][:],
+                in_=W[m][g * 512:(g + 1) * 512, hh * HW:(hh + 1) * HW].rearrange("(p j) w -> p j w", j=4),
+            )
+
+        def load_h(u):
+            t, kp = u // KP, u % KP
+            h_raw[u] = raw.tile([P, 2, 1024], BF16, name="h_raw", tag="h_raw", bufs=H_BUFS)
+            nc.sync.dma_start(out=h_raw[u][:], in_=child_h[t * P:(t + 1) * P, 2 * kp:2 * kp + 2, :])
+
+        def load_c(u):
+            t, kp = u // KP, u % KP
+            c_raw[u] = raw.tile([P, 2, 1024], BF16, name="c_raw%d" % u)
+            nc.sync.dma_start(out=c_raw[u][:], in_=child_c[t * P:(t + 1) * P, 2 * kp:2 * kp + 2, :])
+
+        late_w = [(0, 0, 1), (0, 1, 1), (1, 0, 1), (1, 1, 1)]
+        load_x(0)
+        load_h(0)
+        load_w(0, 0, 0)
+        load_w(0, 1, 0)
+        nc.sync.dma_start(out=brow[0:1, :], in_=bWf.rearrange("(o n) -> o n", o=1))
+        nc.sync.dma_start(out=brow[1:2, :], in_=bUf.rearrange("(o n) -> o n", o=1))
+        load_w(1, 0, 0)
+        load_w(1, 1, 0)
+        load_h(1)
+        load_h(2)
+        load_x(1)
+        load_c(0)
+        load_h(3)
+        load_c(1)
+        load_h(4)
+        load_h(5)
+        load_w(*late_w[0])
+        load_c(2)
+        load_h(6)
+        load_w(*late_w[1])
+        load_c(3)
+        load_h(7)
+        load_w(*late_w[2])
+        load_c(4)
+        load_w(*late_w[3])
+        load_c(5)
+        load_c(6)
+        load_c(7)
+
+        w_grps = {}
+        w_codes = {}
+        w_scales = {}
+        a_grps = {}
+        a_tps = {}
+        a_codes = {}
+        a_scales = {}
+
+        def w_alloc(key):
+            w_grps[key] = grp.tile([P, HW, 4], BF16, name="w_grp", tag="w_grp", bufs=4, align_bytes=64)
+
+        def w_copy(key, eng, c0, c1):
+            if c1 <= c0:
+                return
+            if COPY4:
+                src = w_raw[key][:, :, c0:c1].rearrange("p t (c i) -> p c t i", i=4)
+                dst = w_grps[key][:, c0:c1, :].rearrange("p (c i) t -> p c t i", i=4)
+            else:
+                src = w_raw[key][:].rearrange("p j w -> p w j")[:, c0:c1, :]
+                dst = w_grps[key][:, c0:c1, :]
+            if eng == "v":
+                nc.vector.tensor_copy(out=dst, in_=src)
+            elif eng == "s":
+                nc.scalar.copy(out=dst, in_=src)
+            else:
+                nc.gpsimd.tensor_scalar(out=dst, in0=src, scalar1=1.0, scalar2=0.0, op0=ALU.mult, op1=ALU.add)
+
+        def w_copy_split(key, split):
+            w_alloc(key)
+            v, s, g = split
+            w_copy(key, "v", 0, v)
+            w_copy(key, "s", v, v + s)
+            w_copy(key, "g", v + s, v + s + g)
+
+        def w_quant(key):
+            cd = codes.tile([P, HW], U32, name="wc%d%d%d" % key, align_bytes=64)
+            sc = codes.tile([P, HW], U8, name="ws%d%d%d" % key, align_bytes=64)
+            nc.vector.quantize_mx(out=cd[:].bitcast(FP8X4), scales=sc[:], in_=w_grps[key][:].rearrange("p w j -> p (w j)"))
+            w_codes[key] = cd
+            w_scales[key] = sc
+
+        def rows_of(key):
+            if key[0] == "x":
+                return [x_raw[key[1]][:]]
+            return [h_raw[key[1]][:, 0, :], h_raw[key[1]][:, 1, :]]
+
+        def a_transpose(key):
+            tps = []
+            for src in rows_of(key):
+                words = src.bitcast(F32)
+                tp = psum.tile([P, 4, P], F32, name="tp", tag="tp", bufs=4)
+                for g in range(G):
+                    for e in range(2):
+                        nc.tensor.transpose(tp[:, 2 * g + e, :], words[:, 256 * g + e:256 * (g + 1):2], ident[:])
+                tps.append(tp)
+            a_tps[key] = tps
+
+        def a_evac(key, on_vector=False):
+            ns = len(a_tps[key])
+            a_grp = grp.tile([P, G * ns * P * 4], BF16, name="a_grp%d" % ns, tag="a_grp%d" % ns, bufs=(2 if ns == 1 else 4), align_bytes=64)
+            gw = a_grp[:].bitcast(F32).rearrange("p (g s r e) -> p g s r e", g=G, s=ns, r=P, e=2)
+            for s in range(ns):
+                src = a_tps[key][s][:].rearrange("p (g e) r -> p g r e", g=G, e=2)
+                if on_vector:
+                    nc.vector.tensor_copy(out=gw[:, :, s, :, :], in_=src)
+                else:
+                    nc.scalar.copy(out=gw[:, :, s, :, :], in_=src)
+            a_grps[key] = a_grp
+
+        def a_quant(key):
+            ns = len(a_tps[key])
+            cd = codes.tile([P, G * ns * P], U32, name="ac%s%d" % key, align_bytes=64)
+            sc = codes.tile([P, G * ns * P], U8, name="as%s%d" % key, align_bytes=64)
+            nc.vector.quantize_mx(out=cd[:].bitcast(FP8X4), scales=sc[:], in_=a_grps[key][:])
+            a_codes[key] = cd
+            a_scales[key] = sc
+
+        def mx_group(acc, key, ns, s, m, hh):
+            for g in range(G):
+                c0 = (g * ns + s) * P
+                nc.tensor.matmul_mx(
+                    out=acc[:],
+                    lhsT=a_codes[key][:, c0:c0 + P].bitcast(FP8X4),
+                    lhsT_scale=a_scales[key][:, c0:c0 + P],
+                    rhs=w_codes[(m, g, hh)][:].bitcast(FP8X4),
+                    rhs_scale=w_scales[(m, g, hh)][:],
+                    start=(g == 0),
+                    stop=(g == G - 1),
+                )
+
+        bias_sb = const.tile([P, 2 * HW], F32, name="bias_sb")
+
+        def make_bias(hh):
+            bp = psum.tile([P, HW], F32, name="bp", tag="acc", bufs=ACC_BUFS)
+            nc.tensor.matmul(out=bp[:], lhsT=ones[:], rhs=brow[:, hh * HW:(hh + 1) * HW], start=True, stop=True)
+            nc.scalar.copy(out=bias_sb[:, hh * HW:(hh + 1) * HW], in_=bp[:])
+
+        xfbs = {}
+        zts = {}
+
+        def where(i):
+            q = i // KP
+            hh, t = q // 2, q % 2
+            return q, hh, t, t * KP + i % KP
+
+        def xf(q):
+            hh, t = q // 2, q % 2
+            xacc = psum.tile([P, HW], F32, name="xacc", tag="acc", bufs=ACC_BUFS)
+            mx_group(xacc, ("x", t), 1, 0, 0, hh)
+            xfb = ep.tile([P, HW], F32, name="xfb", tag="xfb", bufs=2)
+            nc.vector.tensor_tensor(out=xfb[:], in0=xacc[:], in1=bias_sb[:, hh * HW:(hh + 1) * HW], op=ALU.add)
+            xfbs[q] = xfb
+
+        def mm_add(i):
+            q, hh, t, u = where(i)
+            zt = ep.tile([P, 2, HW], F32, name="zt", tag="zt", bufs=ZT_BUFS)
+            for s in range(2):
+                acc = psum.tile([P, HW], F32, name="acc", tag="acc", bufs=ACC_BUFS)
+                mx_group(acc, ("h", u), 2, s, 1, hh)
+                nc.vector.tensor_tensor(out=zt[:, s, :], in0=acc[:], in1=xfbs[q][:], op=ALU.add)
+            zts[i] = zt
+
+        def sigm(i):
+            nc.scalar.activation(out=zts[i][:], in_=zts[i][:], func=ACT.Sigmoid)
+
+        def prod_v(i):
+            q, hh, t, u = where(i)
+            a = V_COLS if (G_PROD and i >= G_FROM and i not in G_BUSY and not (FAST_TAIL and i == NSTEP - 1)) else HW
+            nc.vector.tensor_tensor(out=zts[i][:, :, 0:a], in0=zts[i][:, :, 0:a], in1=c_raw[u][:, :, hh * HW:hh * HW + a], op=ALU.mult)
+
+        def prod_v_half(i, s):
+            q, hh, t, u = where(i)
+            nc.vector.tensor_tensor(out=zts[i][:, s, :], in0=zts[i][:, s, :], in1=c_raw[u][:, s, hh * HW:(hh + 1) * HW], op=ALU.mult)
+
+        def prod_g(i):
+            q, hh, t, u = where(i)
+            if (FAST_TAIL and i == NSTEP - 1) or i in G_BUSY:
+                return
+            if i >= 1:
+                nc.gpsimd.tensor_copy(out=gdum[:, i:i + 1], in_=zts[i - 1][:, 0, 0:1])
+            nc.gpsimd.tensor_tensor(out=zts[i][:, :, V_COLS:HW], in0=zts[i][:, :, V_COLS:HW], in1=c_raw[u][:, :, hh * HW + V_COLS:(hh + 1) * HW], op=ALU.mult)
+
+        oTs_ps = {}
+        oTs_sb = {}
+        o2s = {}
+
+        def f1(q, j):
+            if j == 0:
+                oTs_ps[q] = psum.tile([P, 4, P], F32, name="oT", tag="oT", bufs=1)
+            for k in range(8):
+                nc.tensor.matmul(
+                    out=oTs_ps[q][:, j, :],
+                    lhsT=zts[4 * q + k // 2][:, k % 2, j * P:(j + 1) * P],
+                    rhs=ident[:],
+                    is_transpose=True,
+                    start=(k == 0),
+                    stop=(k == 7),
+                )
+
+        last_acc = []
+
+        def f1_last(i):
+            if i == 12:
+                for j in range(4):
+                    last_acc.append(psum.tile([P, 4, P], F32, name="la%d" % j, tag="tp", bufs=4))
+            for j in range(4):
+                for s in range(2):
+                    k = 2 * (i - 12) + s
+                    nc.tensor.matmul(
+                        out=last_acc[j][:, 0, :],
+                        lhsT=zts[i][:, s, j * P:(j + 1) * P],
+                        rhs=ident[:],
+                        is_transpose=True,
+                        start=(k == 0),
+                        stop=(k == 7),
+                    )
+
+        def f1_last_half(i, s):
+            k = 2 * (i - 12) + s
+            for j in range(4):
+                nc.tensor.matmul(
+                    out=last_acc[j][:, 0, :],
+                    lhsT=zts[i][:, s, j * P:(j + 1) * P],
+                    rhs=ident[:],
+                    is_transpose=True,
+                    start=(k == 0),
+                    stop=(k == 7),
+                )
+
+        def f1e_last():
+            oa = ep.tile([P, 2, P], F32, name="oTa", tag="oTa", bufs=1)
+            ob = ep.tile([P, 2, P], F32, name="oTb", tag="oTb", bufs=1)
+            for j in range(2):
+                nc.scalar.copy(out=oa[:, j, :], in_=last_acc[j][:, 0, :])
+                nc.vector.tensor_copy(out=ob[:, j, :], in_=last_acc[2 + j][:, 0, :])
+            oTs_sb[3] = [oa[:, 0, :], oa[:, 1, :], ob[:, 0, :], ob[:, 1, :]]
+
+        def f1e(q):
+            oTs = ep.tile([P, 4, P], F32, name="oTs", tag="oTs", bufs=2)
+            nc.scalar.copy(out=oTs[:], in_=oTs_ps[q][:])
+            oTs_sb[q] = [oTs[:, j, :] for j in range(4)]
+
+        def f2(q):
+            o2 = psum.tile([P, 4, P], F32, name="o2", tag="acc", bufs=ACC_BUFS)
+            for j in range(4):
+                nc.tensor.transpose(o2[:, j, :], oTs_sb[q][j], ident[:])
+            o2s[q] = o2
+
+        def f2e(q, last):
+            hh, t = q // 2, q % 2
+            rows = slice(t * P, (t + 1) * P)
+            cols = slice(hh * HW, (hh + 1) * HW)
+            o_sb = ep.tile([P, HW], F32, name="o_sb", tag="o_sb", bufs=2)
+            o8 = ep.tile([P, HW], FP8, name="o8", tag="o8", bufs=2)
+            o2f = o2s[q][:].rearrange("p j n -> p (j n)")
+            if last:
+                nc.vector.tensor_copy(out=o_sb[:], in_=o2f)
+            else:
+                nc.scalar.copy(out=o_sb[:], in_=o2f)
+            nc.scalar.activation(out=o8[:], in_=o2f, func=ACT.Copy, scale=Y_SCALE, saturate=False)
+            nc.sync.dma_start(out=out_0[rows, cols], in_=o_sb[:])
+            nc.sync.dma_start(out=out_1[rows, cols], in_=o8[:].bitcast(U8))
+
+        a_transpose(("x", 0))
+        a_evac(("x", 0), HEAD_EVAC_V)
+        a_transpose(("h", 0))
+        a_evac(("h", 0), HEAD_EVAC_V)
+        a_quant(("x", 0))
+        w_copy_split((0, 0, 0), HEAD_SPLIT)
+        a_quant(("h", 0))
+        w_copy_split((0, 1, 0), HEAD_SPLIT)
+        w_quant((0, 0, 0))
+        make_bias(0)
+        w_copy_split((1, 0, 0), HEAD_SPLIT)
+        w_quant((0, 1, 0))
+        xf(0)
+        w_copy_split((1, 1, 0), HEAD_SPLIT)
+        w_quant((1, 0, 0))
+        for u in range(1, PF):
+            a_transpose(("h", u))
+            a_evac(("h", u), HEAD_EVAC_V)
+        w_quant((1, 1, 0))
+        make_bias(1)
+
+        pe_extra = {}
+        for q in range(3):
+            for j in range(4):
+                pe_extra.setdefault(4 * q + 4 + LAG + (j * F1_STEPS) // 4, []).append((q, j))
+        s_pieces = {}
+        for n in range(4):
+            v, s, g = LATE_SPLIT
+            cuts = list(range(v, v + s, LATE_PIECE)) + [v + s]
+            s_pieces[3 + n] = [(late_w[n], cuts[a], cuts[a + 1]) for a in range(len(cuts) - 1)]
+        for i in range(NSTEP + LAG):
+            if i < NSTEP:
+                if i % KP == KP - 1 and i + 1 < NSTEP:
+                    xf(i // KP + 1)
+                mm_add(i)
+            if G_PROD and G_FROM + LAG <= i:
+                prod_g(i - LAG)
+            if 3 <= i < 7 and LATE_SPLIT[2] > 0:
+                w_alloc(late_w[i - 3])
+                nc.gpsimd.tensor_copy(out=gdum[:, i:i + 1], in_=zts[i - 1 - LAG][:, 0, 0:1])
+                w_copy(late_w[i - 3], "g", LATE_SPLIT[0] + LATE_SPLIT[1], HW)
+            if i - LAG - 1 >= 12:
+                f1_last(i - LAG - 1)
+            if i == 1:
+                a_transpose(("x", 1))
+                a_evac(("x", 1))
+            if i + PF < 8:
+                a_transpose(("h", i + PF))
+            if i == 0:
+                for u in range(1, QF):
+                    a_quant(("h", u))
+            if i + QF < 8:
+                a_quant(("h", i + QF))
+            if i == 2:
+                a_quant(("x", 1))
+            if i < NSTEP and not (FAST_TAIL and i == NSTEP - 1):
+                sigm(i)
+            if i + PF < 8:
+                a_evac(("h", i + PF))
+            if 3 <= i < 7:
+                if LATE_SPLIT[2] == 0:
+                    w_alloc(late_w[i - 3])
+                w_copy(late_w[i - 3], "v", 0, LATE_SPLIT[0])
+                for (key, c0, c1) in s_pieces[i]:
+                    w_copy(key, "s", c0, c1)
+            if 4 <= i < 8:
+                w_quant(late_w[i - 4])
+            if i >= LAG and not (FAST_TAIL and i - LAG == NSTEP - 1):
+                prod_v(i - LAG)
+            if FAST_TAIL and i == NSTEP - 1:
+                for s in range(2):
+                    nc.scalar.activation(out=zts[i][:, s, :], in_=zts[i][:, s, :], func=ACT.Sigmoid)
+            for (q, j) in pe_extra.get(i, []):
+                f1(q, j)
+                if j == 3:
+                    f1e(q)
+            for q in range(3):
+                if i == 4 * q + 4 + LAG + F1_STEPS + F2_DELAY:
+                    f2(q)
+                    f2e(q, False)
+        for q in range(3):
+            if 4 * q + 4 + LAG + F1_STEPS + F2_DELAY > NSTEP + LAG - 1:
+                f2(q)
+                f2e(q, False)
+        if FAST_TAIL:
+            for s in range(2):
+                prod_v_half(NSTEP - 1, s)
+                f1_last_half(NSTEP - 1, s)
+        else:
+            f1_last(15)
+        f1e_last()
+        f2(3)
+        f2e(3, True)

@@ -21,7 +21,7 @@ HW = 512
 Y_SCALE = 270.0
 NSTEP = 16
 
-HEAD_SPLIT = [256,256,0]
+HEAD_SPLIT = [320,192,0]
 LATE_SPLIT = [192,320,0]
 LATE_PIECE = 512
 G_PROD = True
@@ -39,8 +39,12 @@ PE_LATE = False
 PE_EVAC = ["v","v"]
 G_BUSY = [i - LAG for i in range(3, 7)] if LATE_SPLIT[2] > 0 else []
 QF = 2
-F2_DELAY = 1
+F2_DELAY = 0
 H_BUFS = 6
+TLAG = 2
+INC_FROM = 1
+V_FIN = [3]
+EVAC_FIRST = True
 
 
 def tile_childsumtreelstmcell_pa_kernel(tc, x, child_h, child_c, Wf, bWf, Uf, bUf, out_0, out_1):
@@ -93,13 +97,13 @@ def tile_childsumtreelstmcell_pa_kernel(tc, x, child_h, child_c, Wf, bWf, Uf, bU
             nc.sync.dma_start(out=c_raw[u][:], in_=child_c[t * P:(t + 1) * P, 2 * kp:2 * kp + 2, :])
 
         late_w = [(0, 0, 1), (0, 1, 1), (1, 0, 1), (1, 1, 1)]
-        load_x(0)
-        load_h(0)
         load_w(0, 0, 0)
+        load_x(0)
         load_w(0, 1, 0)
+        load_h(0)
+        load_w(1, 0, 0)
         nc.sync.dma_start(out=brow[0:1, :], in_=bWf.rearrange("(o n) -> o n", o=1))
         nc.sync.dma_start(out=brow[1:2, :], in_=bUf.rearrange("(o n) -> o n", o=1))
-        load_w(1, 0, 0)
         load_w(1, 1, 0)
         load_h(1)
         load_h(2)
@@ -281,26 +285,29 @@ def tile_childsumtreelstmcell_pa_kernel(tc, x, child_h, child_c, Wf, bWf, Uf, bU
                     stop=(k == 7),
                 )
 
-        last_acc = []
+        sum_banks = {}
 
         def f1_last(i):
-            if i == 12:
+            if i % KP == 0:
+                sum_banks[i // KP] = []
                 for j in range(4):
-                    last_acc.append(psum.tile([P, 4, P], F32, name="la%d" % j, tag="tp", bufs=4))
+                    sum_banks[i // KP].append(psum.tile([P, 4, P], F32, name="la%d" % j, tag="tp", bufs=4))
+            last_acc = sum_banks[i // KP]
             for j in range(4):
                 for s in range(2):
-                    k = 2 * (i - 12) + s
+                    k = 2 * (i % KP) + s
                     nc.tensor.matmul(
                         out=last_acc[j][:, 0, :],
                         lhsT=zts[i][:, s, j * P:(j + 1) * P],
                         rhs=ident[:],
                         is_transpose=True,
                         start=(k == 0),
-                        stop=(k == 7),
+                        stop=(k == (5 if i // KP in V_FIN else 7)),
                     )
 
         def f1_last_half(i, s):
-            k = 2 * (i - 12) + s
+            k = 2 * (i % KP) + s
+            last_acc = sum_banks[i // KP]
             for j in range(4):
                 nc.tensor.matmul(
                     out=last_acc[j][:, 0, :],
@@ -312,6 +319,7 @@ def tile_childsumtreelstmcell_pa_kernel(tc, x, child_h, child_c, Wf, bWf, Uf, bU
                 )
 
         def f1e_last():
+            last_acc = sum_banks[3]
             oa = ep.tile([P, 2, P], F32, name="oTa", tag="oTa", bufs=1)
             ob = ep.tile([P, 2, P], F32, name="oTb", tag="oTb", bufs=1)
             for j in range(2):
@@ -319,13 +327,19 @@ def tile_childsumtreelstmcell_pa_kernel(tc, x, child_h, child_c, Wf, bWf, Uf, bU
                 nc.vector.tensor_copy(out=ob[:, j, :], in_=last_acc[2 + j][:, 0, :])
             oTs_sb[3] = [oa[:, 0, :], oa[:, 1, :], ob[:, 0, :], ob[:, 1, :]]
 
+        def f1e_inc(q):
+            oTs = ep.tile([P, 4, P], F32, name="oTs", tag="oTs", bufs=2)
+            for j in range(4):
+                nc.scalar.copy(out=oTs[:, j, :], in_=sum_banks[q][j][:, 0, :])
+            oTs_sb[q] = [oTs[:, j, :] for j in range(4)]
+
         def f1e(q):
             oTs = ep.tile([P, 4, P], F32, name="oTs", tag="oTs", bufs=2)
             nc.scalar.copy(out=oTs[:], in_=oTs_ps[q][:])
             oTs_sb[q] = [oTs[:, j, :] for j in range(4)]
 
         def f2(q):
-            o2 = psum.tile([P, 4, P], F32, name="o2", tag="acc", bufs=ACC_BUFS)
+            o2 = psum.tile([P, 4, P], F32, name="o2", tag="oT", bufs=1)
             for j in range(4):
                 nc.tensor.transpose(o2[:, j, :], oTs_sb[q][j], ident[:])
             o2s[q] = o2
@@ -345,29 +359,45 @@ def tile_childsumtreelstmcell_pa_kernel(tc, x, child_h, child_c, Wf, bWf, Uf, bU
             nc.sync.dma_start(out=out_0[rows, cols], in_=o_sb[:])
             nc.sync.dma_start(out=out_1[rows, cols], in_=o8[:].bitcast(U8))
 
+        def fin_add(q, s):
+            i = 4 * q + 3
+            if s == 0:
+                nc.vector.tensor_tensor(out=zts[i][:, 0, :], in0=zts[i][:, 0, :], in1=zts[i][:, 1, :], op=ALU.add)
+            else:
+                hh, t = q // 2, q % 2
+                rows = slice(t * P, (t + 1) * P)
+                cols = slice(hh * HW, (hh + 1) * HW)
+                o_sb = ep.tile([P, HW], F32, name="o_sb", tag="o_sb", bufs=2)
+                o8 = ep.tile([P, HW], FP8, name="o8", tag="o8", bufs=2)
+                nc.vector.tensor_tensor(out=o_sb[:], in0=zts[i][:, 0, :], in1=o2s[q][:].rearrange("p j n -> p (j n)"), op=ALU.add)
+                nc.sync.dma_start(out=out_0[rows, cols], in_=o_sb[:])
+                nc.scalar.activation(out=o8[:], in_=o_sb[:], func=ACT.Copy, scale=Y_SCALE, saturate=False)
+                nc.sync.dma_start(out=out_1[rows, cols], in_=o8[:].bitcast(U8))
+
+        w_copy_split((0, 0, 0), HEAD_SPLIT)
         a_transpose(("x", 0))
         a_evac(("x", 0), HEAD_EVAC_V)
-        a_transpose(("h", 0))
-        a_evac(("h", 0), HEAD_EVAC_V)
-        a_quant(("x", 0))
-        w_copy_split((0, 0, 0), HEAD_SPLIT)
-        a_quant(("h", 0))
         w_copy_split((0, 1, 0), HEAD_SPLIT)
         w_quant((0, 0, 0))
-        make_bias(0)
-        w_copy_split((1, 0, 0), HEAD_SPLIT)
+        a_quant(("x", 0))
+        a_transpose(("h", 0))
+        a_evac(("h", 0), HEAD_EVAC_V)
         w_quant((0, 1, 0))
-        xf(0)
+        w_copy_split((1, 0, 0), HEAD_SPLIT)
+        make_bias(0)
+        a_quant(("h", 0))
         w_copy_split((1, 1, 0), HEAD_SPLIT)
+        xf(0)
         w_quant((1, 0, 0))
         for u in range(1, PF):
             a_transpose(("h", u))
             a_evac(("h", u), HEAD_EVAC_V)
         w_quant((1, 1, 0))
+        a_quant(("h", 1))
         make_bias(1)
 
         pe_extra = {}
-        for q in range(3):
+        for q in range(INC_FROM):
             for j in range(4):
                 pe_extra.setdefault(4 * q + 4 + LAG + (j * F1_STEPS) // 4, []).append((q, j))
         s_pieces = {}
@@ -386,19 +416,20 @@ def tile_childsumtreelstmcell_pa_kernel(tc, x, child_h, child_c, Wf, bWf, Uf, bU
                 w_alloc(late_w[i - 3])
                 nc.gpsimd.tensor_copy(out=gdum[:, i:i + 1], in_=zts[i - 1 - LAG][:, 0, 0:1])
                 w_copy(late_w[i - 3], "g", LATE_SPLIT[0] + LATE_SPLIT[1], HW)
-            if i - LAG - 1 >= 12:
-                f1_last(i - LAG - 1)
-            if i == 1:
+            pe_sum = 4 * INC_FROM <= i - TLAG < NSTEP and not ((i - TLAG) // KP in V_FIN and (i - TLAG) % KP == KP - 1)
+            pe_end = pe_sum and (i - TLAG) % KP == (KP - 2 if (i - TLAG) // KP in V_FIN else KP - 1)
+            if pe_sum:
+                f1_last(i - TLAG)
+            if pe_end and EVAC_FIRST:
+                f1e_inc((i - TLAG) // KP)
+            if i == 0:
                 a_transpose(("x", 1))
                 a_evac(("x", 1))
             if i + PF < 8:
                 a_transpose(("h", i + PF))
-            if i == 0:
-                for u in range(1, QF):
-                    a_quant(("h", u))
             if i + QF < 8:
                 a_quant(("h", i + QF))
-            if i == 2:
+            if i == 1:
                 a_quant(("x", 1))
             if i < NSTEP and not (FAST_TAIL and i == NSTEP - 1):
                 sigm(i)
@@ -421,20 +452,21 @@ def tile_childsumtreelstmcell_pa_kernel(tc, x, child_h, child_c, Wf, bWf, Uf, bU
                 f1(q, j)
                 if j == 3:
                     f1e(q)
-            for q in range(3):
-                if i == 4 * q + 4 + LAG + F1_STEPS + F2_DELAY:
+            if pe_end and not EVAC_FIRST:
+                f1e_inc((i - TLAG) // KP)
+            for q in range(4):
+                if q < INC_FROM and i == 4 * q + 4 + LAG + F1_STEPS + F2_DELAY:
                     f2(q)
                     f2e(q, False)
-        for q in range(3):
-            if 4 * q + 4 + LAG + F1_STEPS + F2_DELAY > NSTEP + LAG - 1:
-                f2(q)
-                f2e(q, False)
-        if FAST_TAIL:
-            for s in range(2):
-                prod_v_half(NSTEP - 1, s)
-                f1_last_half(NSTEP - 1, s)
-        else:
-            f1_last(15)
-        f1e_last()
-        f2(3)
-        f2e(3, True)
+                if q >= INC_FROM and q not in V_FIN and i == 4 * q + 4 + TLAG:
+                    f2(q)
+                    f2e(q, False)
+                if q in V_FIN and i == 4 * q + 2 + TLAG:
+                    f2(q)
+                if q in V_FIN and q < 3 and i == 4 * q + 3 + TLAG:
+                    fin_add(q, 0)
+                    fin_add(q, 1)
+        for s in range(2):
+            prod_v_half(NSTEP - 1, s)
+        for s in range(2):
+            fin_add(3, s)

@@ -45,6 +45,7 @@ TLAG = 2
 INC_FROM = 1
 V_FIN = [3]
 EVAC_FIRST = True
+PAIRED = True
 
 
 def tile_childsumtreelstmcell_pa_kernel(tc, x, child_h, child_c, Wf, bWf, Uf, bUf, out_0, out_1):
@@ -416,12 +417,11 @@ def tile_childsumtreelstmcell_pa_kernel(tc, x, child_h, child_c, Wf, bWf, Uf, bU
                 w_alloc(late_w[i - 3])
                 nc.gpsimd.tensor_copy(out=gdum[:, i:i + 1], in_=zts[i - 1 - LAG][:, 0, 0:1])
                 w_copy(late_w[i - 3], "g", LATE_SPLIT[0] + LATE_SPLIT[1], HW)
-            pe_sum = 4 * INC_FROM <= i - TLAG < NSTEP and not ((i - TLAG) // KP in V_FIN and (i - TLAG) % KP == KP - 1)
-            pe_end = pe_sum and (i - TLAG) % KP == (KP - 2 if (i - TLAG) // KP in V_FIN else KP - 1)
-            if pe_sum:
-                f1_last(i - TLAG)
-            if pe_end and EVAC_FIRST:
-                f1e_inc((i - TLAG) // KP)
+            for k in range(4 * INC_FROM, NSTEP - 1):
+                if k + (3 if PAIRED and k % 2 == 0 and k != NSTEP - 2 else 2) == i:
+                    f1_last(k)
+                    if k % KP == (KP - 2 if k // KP in V_FIN else KP - 1):
+                        f1e_inc(k // KP)
             if i == 0:
                 a_transpose(("x", 1))
                 a_evac(("x", 1))
@@ -452,8 +452,6 @@ def tile_childsumtreelstmcell_pa_kernel(tc, x, child_h, child_c, Wf, bWf, Uf, bU
                 f1(q, j)
                 if j == 3:
                     f1e(q)
-            if pe_end and not EVAC_FIRST:
-                f1e_inc((i - TLAG) // KP)
             for q in range(4):
                 if q < INC_FROM and i == 4 * q + 4 + LAG + F1_STEPS + F2_DELAY:
                     f2(q)

@@ -453,10 +453,10 @@ def tile_childsumtreelstmcell_pa_kernel(tc, x, child_h, child_c, Wf, bWf, Uf, bU
                 if j == 3:
                     f1e(q)
             for q in range(4):
-                if q < INC_FROM and i == 4 * q + 4 + LAG + F1_STEPS + F2_DELAY:
+                if q < INC_FROM and i == 9:
                     f2(q)
                     f2e(q, False)
-                if q >= INC_FROM and q not in V_FIN and i == 4 * q + 4 + TLAG:
+                if q >= INC_FROM and q not in V_FIN and i == 4 * q + 5 + TLAG:
                     f2(q)
                     f2e(q, False)
                 if q in V_FIN and i == 4 * q + 2 + TLAG:

@@ -250,7 +250,8 @@ def tile_childsumtreelstmcell_pa_kernel(tc, x, child_h, child_c, Wf, bWf, Uf, bU
             zts[i] = zt
 
         def sigm(i):
-            nc.scalar.activation(out=zts[i][:], in_=zts[i][:], func=ACT.Sigmoid)
+            for s in range(2):
+                nc.scalar.activation(out=zts[i][:, s, :], in_=zts[i][:, s, :], func=ACT.Sigmoid)
 
         def prod_v(i):
             q, hh, t, u = where(i)

@@ -41,6 +41,7 @@ G_BUSY = [i - LAG for i in range(3, 7)] if LATE_SPLIT[2] > 0 else []
 QF = 2
 F2_DELAY = 0
 H_BUFS = 6
+WARM = [4, 3, 3, 3]
 TLAG = 2
 INC_FROM = 1
 V_FIN = [3]
@@ -69,6 +70,8 @@ def tile_childsumtreelstmcell_pa_kernel(tc, x, child_h, child_c, Wf, bWf, Uf, bU
         nc.vector.memset(warm[:], 0.0)
         nc.scalar.activation(out=warm[:, 1:2], in_=warm[:, 0:1], func=ACT.Sigmoid)
         gdum = const.tile([P, NSTEP + 2], F32, name="gdum")
+        zb = const.tile([P, HW], BF16, name="zb")
+        nc.vector.memset(zb[:], 0.0)
 
         x_raw = {}
         w_raw = {}
@@ -376,20 +379,29 @@ def tile_childsumtreelstmcell_pa_kernel(tc, x, child_h, child_c, Wf, bWf, Uf, bU
                 nc.scalar.activation(out=o8[:], in_=o_sb[:], func=ACT.Copy, scale=Y_SCALE, saturate=False)
                 nc.sync.dma_start(out=out_1[rows, cols], in_=o8[:].bitcast(U8))
 
+        def keep_warm(n):
+            wps = psum.tile([P, HW], F32, name="wps", tag="oT", bufs=1)
+            for r in range(n):
+                nc.tensor.matmul(out=wps[:], lhsT=ones[:], rhs=zb[:], start=True, stop=True)
+
         w_copy_split((0, 0, 0), HEAD_SPLIT)
+        keep_warm(WARM[0])
         a_transpose(("x", 0))
+        keep_warm(WARM[1])
         a_evac(("x", 0), HEAD_EVAC_V)
         w_copy_split((0, 1, 0), HEAD_SPLIT)
         w_quant((0, 0, 0))
         a_quant(("x", 0))
         a_transpose(("h", 0))
         a_evac(("h", 0), HEAD_EVAC_V)
+        keep_warm(WARM[2])
         w_quant((0, 1, 0))
         w_copy_split((1, 0, 0), HEAD_SPLIT)
         make_bias(0)
         a_quant(("h", 0))
         w_copy_split((1, 1, 0), HEAD_SPLIT)
         xf(0)
+        keep_warm(WARM[3])
         w_quant((1, 0, 0))
         for u in range(1, PF):
             a_transpose(("h", u))

@@ -33,7 +33,7 @@ LAG = 1
 G_FROM = 0
 PF = 3
 COPY4 = True
-V_COLS = 320
+V_COLS = 384
 FAST_TAIL = True
 PE_LATE = False
 PE_EVAC = ["v","v"]

@@ -33,6 +33,7 @@ LAG = 1
 G_FROM = 0
 PF = 3
 COPY4 = True
+V_COLS_B = 448
 V_COLS = 384
 FAST_TAIL = True
 PE_LATE = False
@@ -258,7 +259,7 @@ def tile_childsumtreelstmcell_pa_kernel(tc, x, child_h, child_c, Wf, bWf, Uf, bU
 
         def prod_v(i):
             q, hh, t, u = where(i)
-            a = V_COLS if (G_PROD and i >= G_FROM and i not in G_BUSY and not (FAST_TAIL and i == NSTEP - 1)) else HW
+            a = (V_COLS if i < 8 else V_COLS_B) if (G_PROD and i >= G_FROM and i not in G_BUSY and not (FAST_TAIL and i == NSTEP - 1)) else HW
             nc.vector.tensor_tensor(out=zts[i][:, :, 0:a], in0=zts[i][:, :, 0:a], in1=c_raw[u][:, :, hh * HW:hh * HW + a], op=ALU.mult)
 
         def prod_v_half(i, s):
@@ -271,7 +272,8 @@ def tile_childsumtreelstmcell_pa_kernel(tc, x, child_h, child_c, Wf, bWf, Uf, bU
                 return
             if i >= 1:
                 nc.gpsimd.tensor_copy(out=gdum[:, i:i + 1], in_=zts[i - 1][:, 0, 0:1])
-            nc.gpsimd.tensor_tensor(out=zts[i][:, :, V_COLS:HW], in0=zts[i][:, :, V_COLS:HW], in1=c_raw[u][:, :, hh * HW + V_COLS:(hh + 1) * HW], op=ALU.mult)
+            a = V_COLS if i < 8 else V_COLS_B
+            nc.gpsimd.tensor_tensor(out=zts[i][:, :, a:HW], in0=zts[i][:, :, a:HW], in1=c_raw[u][:, :, hh * HW + a:(hh + 1) * HW], op=ALU.mult)
 
         oTs_ps = {}
         oTs_sb = {}

from contextlib import ExitStack

import concourse.mybir as mybir
from concourse.masks import make_identity

FLOPS = 2 * 2048 * 1024 * 1024 + 2 * 256 * 1024 * 1024

F32 = mybir.dt.float32
BF16 = mybir.dt.bfloat16
U32 = mybir.dt.uint32
U8 = mybir.dt.uint8
FP8X4 = mybir.dt.float8_e4m3fn_x4
FP8 = mybir.dt.float8_e4m3fn
ALU = mybir.AluOpType
ACT = mybir.ActivationFunctionType

P = 128
KP = 4
G = 2
HW = 512
Y_SCALE = 270.0
NSTEP = 16

HEAD_SPLIT = [320,192,0]
LATE_SPLIT = [192,320,0]
LATE_PIECE = 512
G_PROD = True
HEAD_EVAC_V = False
ACC_BUFS = 3
F1_STEPS = 3
ZT_BUFS = 9
LAG = 1
G_FROM = 0
PF = 3
COPY4 = True
V_COLS_B = 448
V_COLS = 384
FAST_TAIL = True
PE_LATE = False
PE_EVAC = ["v","v"]
G_BUSY = [i - LAG for i in range(3, 7)] if LATE_SPLIT[2] > 0 else []
QF = 2
F2_DELAY = 0
H_BUFS = 6
WARM = [4, 3, 3, 3]
TLAG = 2
INC_FROM = 1
V_FIN = [3]
EVAC_FIRST = True
PAIRED = True


def tile_childsumtreelstmcell_pa_kernel(tc, x, child_h, child_c, Wf, bWf, Uf, bUf, out_0, out_1):
    nc = tc.nc
    with ExitStack() as ctx:
        const = ctx.enter_context(tc.tile_pool(name="const", bufs=1))
        raw = ctx.enter_context(tc.tile_pool(name="raw", bufs=1))
        grp = ctx.enter_context(tc.tile_pool(name="grp", bufs=3))
        codes = ctx.enter_context(tc.tile_pool(name="codes", bufs=1))
        ep = ctx.enter_context(tc.tile_pool(name="ep", bufs=2))
        psum = ctx.enter_context(tc.psum_pool(name="psum", bufs=1))
        ctx.enter_context(tc.manual_schedule())

        ident = const.tile([P, P], F32, name="ident")
        make_identity(nc, ident[:])
        ones = const.tile([P, P], BF16, name="ones")
        nc.vector.memset(ones[:], 1.0)
        brow = const.tile([P, 2 * HW], BF16, name="brow")
        nc.gpsimd.memset(brow[:], 0.0)
        warm = const.tile([P, 2], F32, name="warm")
        nc.vector.memset(warm[:], 0.0)
        nc.scalar.activation(out=warm[:, 1:2], in_=warm[:, 0:1], func=ACT.Sigmoid)
        gdum = const.tile([P, NSTEP + 2], F32, name="gdum")
        zb = const.tile([P, HW], BF16, name="zb")
        nc.vector.memset(zb[:], 0.0)

        x_raw = {}
        w_raw = {}
        h_raw = {}
        c_raw = {}
        W = {0: Wf, 1: Uf}

        def load_x(t):
            x_raw[t] = raw.tile([P, 1024], BF16, name="x_raw%d" % t)
            nc.sync.dma_start(out=x_raw[t][:], in_=x[t * P:(t + 1) * P, :])

        def load_w(m, g, hh):
            w_raw[(m, g, hh)] = raw.tile([P, 4, HW], BF16, name="w_raw%d%d%d" % (m, g, hh))
            nc.sync.dma_start(
                out=w_raw[(m, g, hh)][:],
                in_=W[m][g * 512:(g + 1) * 512, hh * HW:(hh + 1) * HW].rearrange("(p j) w -> p j w", j=4),
            )

        def load_h(u):
            t, kp = u // KP, u % KP
            h_raw[u] = raw.tile([P, 2, 1024], BF16, name="h_raw", tag="h_raw", bufs=H_BUFS)
            nc.sync.dma_start(out=h_raw[u][:], in_=child_h[t * P:(t + 1) * P, 2 * kp:2 * kp + 2, :])

        def load_c(u):
            t, kp = u // KP, u % KP
            c_raw[u] = raw.tile([P, 2, 1024], BF16, name="c_raw%d" % u)
            nc.sync.dma_start(out=c_raw[u][:], in_=child_c[t * P:(t + 1) * P, 2 * kp:2 * kp + 2, :])

        late_w = [(0, 0, 1), (0, 1, 1), (1, 0, 1), (1, 1, 1)]
        load_w(0, 0, 0)
        load_x(0)
        load_w(0, 1, 0)
        load_h(0)
        load_w(1, 0, 0)
        nc.sync.dma_start(out=brow[0:1, :], in_=bWf.rearrange("(o n) -> o n", o=1))
        nc.sync.dma_start(out=brow[1:2, :], in_=bUf.rearrange("(o n) -> o n", o=1))
        load_w(1, 1, 0)
        load_h(1)
        load_h(2)
        load_x(1)
        load_c(0)
        load_h(3)
        load_c(1)
        load_h(4)
        load_h(5)
        load_w(*late_w[0])
        load_c(2)
        load_h(6)
        load_w(*late_w[1])
        load_c(3)
        load_h(7)
        load_w(*late_w[2])
        load_c(4)
        load_w(*late_w[3])
        load_c(5)
        load_c(6)
        load_c(7)

        w_grps = {}
        w_codes = {}
        w_scales = {}
        a_grps = {}
        a_tps = {}
        a_codes = {}
        a_scales = {}

        def w_alloc(key):
            w_grps[key] = grp.tile([P, HW, 4], BF16, name="w_grp", tag="w_grp", bufs=4, align_bytes=64)

        def w_copy(key, eng, c0, c1):
            if c1 <= c0:
                return
            if COPY4:
                src = w_raw[key][:, :, c0:c1].rearrange("p t (c i) -> p c t i", i=4)
                dst = w_grps[key][:, c0:c1, :].rearrange("p (c i) t -> p c t i", i=4)
            else:
                src = w_raw[key][:].rearrange("p j w -> p w j")[:, c0:c1, :]
                dst = w_grps[key][:, c0:c1, :]
            if eng == "v":
                nc.vector.tensor_copy(out=dst, in_=src)
            elif eng == "s":
                nc.scalar.copy(out=dst, in_=src)
            else:
                nc.gpsimd.tensor_scalar(out=dst, in0=src, scalar1=1.0, scalar2=0.0, op0=ALU.mult, op1=ALU.add)

        def w_copy_split(key, split):
            w_alloc(key)
            v, s, g = split
            w_copy(key, "v", 0, v)
            w_copy(key, "s", v, v + s)
            w_copy(key, "g", v + s, v + s + g)

        def w_quant(key):
            cd = codes.tile([P, HW], U32, name="wc%d%d%d" % key, align_bytes=64)
            sc = codes.tile([P, HW], U8, name="ws%d%d%d" % key, align_bytes=64)
            nc.vector.quantize_mx(out=cd[:].bitcast(FP8X4), scales=sc[:], in_=w_grps[key][:].rearrange("p w j -> p (w j)"))
            w_codes[key] = cd
            w_scales[key] = sc

        def rows_of(key):
            if key[0] == "x":
                return [x_raw[key[1]][:]]
            return [h_raw[key[1]][:, 0, :], h_raw[key[1]][:, 1, :]]

        def a_transpose(key):
            tps = []
            for src in rows_of(key):
                words = src.bitcast(F32)
                tp = psum.tile([P, 4, P], F32, name="tp", tag="tp", bufs=4)
                for g in range(G):
                    for e in range(2):
                        nc.tensor.transpose(tp[:, 2 * g + e, :], words[:, 256 * g + e:256 * (g + 1):2], ident[:])
                tps.append(tp)
            a_tps[key] = tps

        def a_evac(key, on_vector=False):
            ns = len(a_tps[key])
            a_grp = grp.tile([P, G * ns * P * 4], BF16, name="a_grp%d" % ns, tag="a_grp%d" % ns, bufs=(2 if ns == 1 else 4), align_bytes=64)
            gw = a_grp[:].bitcast(F32).rearrange("p (g s r e) -> p g s r e", g=G, s=ns, r=P, e=2)
            for s in range(ns):
                src = a_tps[key][s][:].rearrange("p (g e) r -> p g r e", g=G, e=2)
                if on_vector:
                    nc.vector.tensor_copy(out=gw[:, :, s, :, :], in_=src)
                else:
                    nc.scalar.copy(out=gw[:, :, s, :, :], in_=src)
            a_grps[key] = a_grp

        def a_quant(key):
            ns = len(a_tps[key])
            cd = codes.tile([P, G * ns * P], U32, name="ac%s%d" % key, align_bytes=64)
            sc = codes.tile([P, G * ns * P], U8, name="as%s%d" % key, align_bytes=64)
            nc.vector.quantize_mx(out=cd[:].bitcast(FP8X4), scales=sc[:], in_=a_grps[key][:])
            a_codes[key] = cd
            a_scales[key] = sc

        def mx_group(acc, key, ns, s, m, hh):
            for g in range(G):
                c0 = (g * ns + s) * P
                nc.tensor.matmul_mx(
                    out=acc[:],
                    lhsT=a_codes[key][:, c0:c0 + P].bitcast(FP8X4),
                    lhsT_scale=a_scales[key][:, c0:c0 + P],
                    rhs=w_codes[(m, g, hh)][:].bitcast(FP8X4),
                    rhs_scale=w_scales[(m, g, hh)][:],
                    start=(g == 0),
                    stop=(g == G - 1),
                )

        bias_sb = const.tile([P, 2 * HW], F32, name="bias_sb")

        def make_bias(hh):
            bp = psum.tile([P, HW], F32, name="bp", tag="acc", bufs=ACC_BUFS)
            nc.tensor.matmul(out=bp[:], lhsT=ones[:], rhs=brow[:, hh * HW:(hh + 1) * HW], start=True, stop=True)
            nc.scalar.copy(out=bias_sb[:, hh * HW:(hh + 1) * HW], in_=bp[:])

        xfbs = {}
        zts = {}

        def where(i):
            q = i // KP
            hh, t = q // 2, q % 2
            return q, hh, t, t * KP + i % KP

        def xf(q):
            hh, t = q // 2, q % 2
            xacc = psum.tile([P, HW], F32, name="xacc", tag="acc", bufs=ACC_BUFS)
            mx_group(xacc, ("x", t), 1, 0, 0, hh)
            xfb = ep.tile([P, HW], F32, name="xfb", tag="xfb", bufs=2)
            nc.vector.tensor_tensor(out=xfb[:], in0=xacc[:], in1=bias_sb[:, hh * HW:(hh + 1) * HW], op=ALU.add)
            xfbs[q] = xfb

        def mm_add(i):
            q, hh, t, u = where(i)
            zt = ep.tile([P, 2, HW], F32, name="zt", tag="zt", bufs=ZT_BUFS)
            for s in range(2):
                acc = psum.tile([P, HW], F32, name="acc", tag="acc", bufs=ACC_BUFS)
                mx_group(acc, ("h", u), 2, s, 1, hh)
                nc.vector.tensor_tensor(out=zt[:, s, :], in0=acc[:], in1=xfbs[q][:], op=ALU.add)
            zts[i] = zt

        def sigm(i):
            for s in range(2):
                nc.scalar.activation(out=zts[i][:, s, :], in_=zts[i][:, s, :], func=ACT.Sigmoid)

        def prod_v(i):
            q, hh, t, u = where(i)
            a = (V_COLS if i < 8 else V_COLS_B) if (G_PROD and i >= G_FROM and i not in G_BUSY and not (FAST_TAIL and i == NSTEP - 1)) else HW
            nc.vector.tensor_tensor(out=zts[i][:, :, 0:a], in0=zts[i][:, :, 0:a], in1=c_raw[u][:, :, hh * HW:hh * HW + a], op=ALU.mult)

        def prod_v_half(i, s):
            q, hh, t, u = where(i)
            nc.vector.tensor_tensor(out=zts[i][:, s, :], in0=zts[i][:, s, :], in1=c_raw[u][:, s, hh * HW:(hh + 1) * HW], op=ALU.mult)

        def prod_g(i):
            q, hh, t, u = where(i)
            if (FAST_TAIL and i == NSTEP - 1) or i in G_BUSY:
                return
            if i >= 1:
                nc.gpsimd.tensor_copy(out=gdum[:, i:i + 1], in_=zts[i - 1][:, 0, 0:1])
            a = V_COLS if i < 8 else V_COLS_B
            nc.gpsimd.tensor_tensor(out=zts[i][:, :, a:HW], in0=zts[i][:, :, a:HW], in1=c_raw[u][:, :, hh * HW + a:(hh + 1) * HW], op=ALU.mult)

        oTs_ps = {}
        oTs_sb = {}
        o2s = {}

        def f1(q, j):
            if j == 0:
                oTs_ps[q] = psum.tile([P, 4, P], F32, name="oT", tag="oT", bufs=1)
            for k in range(8):
                nc.tensor.matmul(
                    out=oTs_ps[q][:, j, :],
                    lhsT=zts[4 * q + k // 2][:, k % 2, j * P:(j + 1) * P],
                    rhs=ident[:],
                    is_transpose=True,
                    start=(k == 0),
                    stop=(k == 7),
                )

        sum_banks = {}

        def f1_last(i):
            if i % KP == 0:
                sum_banks[i // KP] = []
                for j in range(4):
                    sum_banks[i // KP].append(psum.tile([P, 4, P], F32, name="la%d" % j, tag="tp", bufs=4))
            last_acc = sum_banks[i // KP]
            for j in range(4):
                for s in range(2):
                    k = 2 * (i % KP) + s
                    nc.tensor.matmul(
                        out=last_acc[j][:, 0, :],
                        lhsT=zts[i][:, s, j * P:(j + 1) * P],
                        rhs=ident[:],
                        is_transpose=True,
                        start=(k == 0),
                        stop=(k == (5 if i // KP in V_FIN else 7)),
                    )

        def f1_last_half(i, s):
            k = 2 * (i % KP) + s
            last_acc = sum_banks[i // KP]
            for j in range(4):
                nc.tensor.matmul(
                    out=last_acc[j][:, 0, :],
                    lhsT=zts[i][:, s, j * P:(j + 1) * P],
                    rhs=ident[:],
                    is_transpose=True,
                    start=(k == 0),
                    stop=(k == 7),
                )

        def f1e_last():
            last_acc = sum_banks[3]
            oa = ep.tile([P, 2, P], F32, name="oTa", tag="oTa", bufs=1)
            ob = ep.tile([P, 2, P], F32, name="oTb", tag="oTb", bufs=1)
            for j in range(2):
                nc.scalar.copy(out=oa[:, j, :], in_=last_acc[j][:, 0, :])
                nc.vector.tensor_copy(out=ob[:, j, :], in_=last_acc[2 + j][:, 0, :])
            oTs_sb[3] = [oa[:, 0, :], oa[:, 1, :], ob[:, 0, :], ob[:, 1, :]]

        def f1e_inc(q):
            oTs = ep.tile([P, 4, P], F32, name="oTs", tag="oTs", bufs=2)
            for j in range(4):
                nc.scalar.copy(out=oTs[:, j, :], in_=sum_banks[q][j][:, 0, :])
            oTs_sb[q] = [oTs[:, j, :] for j in range(4)]

        def f1e(q):
            oTs = ep.tile([P, 4, P], F32, name="oTs", tag="oTs", bufs=2)
            nc.scalar.copy(out=oTs[:], in_=oTs_ps[q][:])
            oTs_sb[q] = [oTs[:, j, :] for j in range(4)]

        def f2(q):
            o2 = psum.tile([P, 4, P], F32, name="o2", tag="oT", bufs=1)
            for j in range(4):
                nc.tensor.transpose(o2[:, j, :], oTs_sb[q][j], ident[:])
            o2s[q] = o2

        def f2e(q, last):
            hh, t = q // 2, q % 2
            rows = slice(t * P, (t + 1) * P)
            cols = slice(hh * HW, (hh + 1) * HW)
            o_sb = ep.tile([P, HW], F32, name="o_sb", tag="o_sb", bufs=2)
            o8 = ep.tile([P, HW], FP8, name="o8", tag="o8", bufs=2)
            o2f = o2s[q][:].rearrange("p j n -> p (j n)")
            if last:
                nc.vector.tensor_copy(out=o_sb[:], in_=o2f)
            else:
                nc.scalar.copy(out=o_sb[:], in_=o2f)
            nc.scalar.activation(out=o8[:], in_=o2f, func=ACT.Copy, scale=Y_SCALE, saturate=False)
            nc.sync.dma_start(out=out_0[rows, cols], in_=o_sb[:])
            nc.sync.dma_start(out=out_1[rows, cols], in_=o8[:].bitcast(U8))

        def fin_add(q, s):
            i = 4 * q + 3
            if s == 0:
                nc.vector.tensor_tensor(out=zts[i][:, 0, :], in0=zts[i][:, 0, :], in1=zts[i][:, 1, :], op=ALU.add)
            else:
                hh, t = q // 2, q % 2
                rows = slice(t * P, (t + 1) * P)
                cols = slice(hh * HW, (hh + 1) * HW)
                o_sb = ep.tile([P, HW], F32, name="o_sb", tag="o_sb", bufs=2)
                o8 = ep.tile([P, HW], FP8, name="o8", tag="o8", bufs=2)
                nc.vector.tensor_tensor(out=o_sb[:], in0=zts[i][:, 0, :], in1=o2s[q][:].rearrange("p j n -> p (j n)"), op=ALU.add)
                nc.sync.dma_start(out=out_0[rows, cols], in_=o_sb[:])
                nc.scalar.activation(out=o8[:], in_=o_sb[:], func=ACT.Copy, scale=Y_SCALE, saturate=False)
                nc.sync.dma_start(out=out_1[rows, cols], in_=o8[:].bitcast(U8))

        def keep_warm(n):
            wps = psum.tile([P, HW], F32, name="wps", tag="oT", bufs=1)
            for r in range(n):
                nc.tensor.matmul(out=wps[:], lhsT=ones[:], rhs=zb[:], start=True, stop=True)

        w_copy_split((0, 0, 0), HEAD_SPLIT)
        keep_warm(WARM[0])
        a_transpose(("x", 0))
        keep_warm(WARM[1])
        a_evac(("x", 0), HEAD_EVAC_V)
        w_copy_split((0, 1, 0), HEAD_SPLIT)
        w_quant((0, 0, 0))
        a_quant(("x", 0))
        a_transpose(("h", 0))
        a_evac(("h", 0), HEAD_EVAC_V)
        keep_warm(WARM[2])
        w_quant((0, 1, 0))
        w_copy_split((1, 0, 0), HEAD_SPLIT)
        make_bias(0)
        a_quant(("h", 0))
        w_copy_split((1, 1, 0), HEAD_SPLIT)
        xf(0)
        keep_warm(WARM[3])
        w_quant((1, 0, 0))
        for u in range(1, PF):
            a_transpose(("h", u))
            a_evac(("h", u), HEAD_EVAC_V)
        w_quant((1, 1, 0))
        a_quant(("h", 1))
        make_bias(1)

        pe_extra = {}
        for q in range(INC_FROM):
            for j in range(4):
                pe_extra.setdefault(4 * q + 4 + LAG + (j * F1_STEPS) // 4, []).append((q, j))
        s_pieces = {}
        for n in range(4):
            v, s, g = LATE_SPLIT
            cuts = list(range(v, v + s, LATE_PIECE)) + [v + s]
            s_pieces[3 + n] = [(late_w[n], cuts[a], cuts[a + 1]) for a in range(len(cuts) - 1)]
        for i in range(NSTEP + LAG):
            if i < NSTEP:
                if i % KP == KP - 1 and i + 1 < NSTEP:
                    xf(i // KP + 1)
                mm_add(i)
            if G_PROD and G_FROM + LAG <= i:
                prod_g(i - LAG)
            if 3 <= i < 7 and LATE_SPLIT[2] > 0:
                w_alloc(late_w[i - 3])
                nc.gpsimd.tensor_copy(out=gdum[:, i:i + 1], in_=zts[i - 1 - LAG][:, 0, 0:1])
                w_copy(late_w[i - 3], "g", LATE_SPLIT[0] + LATE_SPLIT[1], HW)
            for k in range(4 * INC_FROM, NSTEP - 1):
                if k + (3 if PAIRED and k % 2 == 0 and k != NSTEP - 2 else 2) == i:
                    f1_last(k)
                    if k % KP == (KP - 2 if k // KP in V_FIN else KP - 1):
                        f1e_inc(k // KP)
            if i == 0:
                a_transpose(("x", 1))
                a_evac(("x", 1))
            if i + PF < 8:
                a_transpose(("h", i + PF))
            if i + QF < 8:
                a_quant(("h", i + QF))
            if i == 1:
                a_quant(("x", 1))
            if i < NSTEP and not (FAST_TAIL and i == NSTEP - 1):
                sigm(i)
            if i + PF < 8:
                a_evac(("h", i + PF))
            if 3 <= i < 7:
                if LATE_SPLIT[2] == 0:
                    w_alloc(late_w[i - 3])
                w_copy(late_w[i - 3], "v", 0, LATE_SPLIT[0])
                for (key, c0, c1) in s_pieces[i]:
                    w_copy(key, "s", c0, c1)
            if 4 <= i < 8:
                w_quant(late_w[i - 4])
            if i >= LAG and not (FAST_TAIL and i - LAG == NSTEP - 1):
                prod_v(i - LAG)
            if FAST_TAIL and i == NSTEP - 1:
                for s in range(2):
                    nc.scalar.activation(out=zts[i][:, s, :], in_=zts[i][:, s, :], func=ACT.Sigmoid)
            for (q, j) in pe_extra.get(i, []):
                f1(q, j)
                if j == 3:
                    f1e(q)
            for q in range(4):
                if q < INC_FROM and i == 9:
                    f2(q)
                    f2e(q, False)
                if q >= INC_FROM and q not in V_FIN and i == 4 * q + 5 + TLAG:
                    f2(q)
                    f2e(q, False)
                if q in V_FIN and i == 4 * q + 2 + TLAG:
                    f2(q)
                if q in V_FIN and q < 3 and i == 4 * q + 3 + TLAG:
                    fin_add(q, 0)
                    fin_add(q, 1)
        for s in range(2):
            prod_v_half(NSTEP - 1, s)
        for s in range(2):
            fin_add(3, s)
